import numpy as np
import ml_dtypes


def mxq(x, axis, fmt="e4m3"):
    dtype, down = {"e4m3": (ml_dtypes.float8_e4m3fn, 7), "e5m2": (ml_dtypes.float8_e5m2, 14)}[fmt]
    v = np.moveaxis(np.asarray(x, np.float32).astype(ml_dtypes.bfloat16).astype(np.float64), axis, -1)
    blocks = v.reshape(v.shape[:-1] + (-1, 32))
    amax = np.abs(blocks).max(-1, keepdims=True)
    byte = np.maximum(np.where(amax > 0, np.frexp(amax)[1] - 1 + 127, 0) - down, 1)
    scale = np.exp2(byte - 127.0)
    codes = (blocks / scale).astype(np.float32).astype(dtype).astype(np.float64)
    return np.moveaxis((codes * scale).reshape(v.shape), -1, axis)


WIDE = False


def mx_kscale(k):
    if not WIDE:
        return np.ones(k)
    levels = np.array([10, -10, 5, -5, 0])
    a = np.random.permutation(np.resize(levels, k // 512 * 4)).reshape(k // 512, 4)
    idx = np.arange(k)
    return np.exp2(a[idx // 512, idx % 128 // 32])


BF16 = ml_dtypes.bfloat16


def bf(x):
    return np.asarray(x, np.float32).astype(BF16)


def f64(x):
    return np.asarray(x).astype(np.float64)


N, T, E, HEADS, LOCAL_ATTN_CTX = 1, 512, 512, 16, 128


def _strided_transpose(x, n_ctx, local_attn_ctx):
    bT_ctx = n_ctx // local_attn_ctx
    n, t, e = x.shape
    x = x.reshape(n, bT_ctx, local_attn_ctx, e)
    x = np.transpose(x, (0, 2, 1, 3))
    return x.reshape(n, t, e)


def setup_inputs():
    s = mx_kscale(E)
    g = 1.2 / HEADS ** 0.25
    return {"q": bf(np.random.standard_normal((N, T, E)) * g * s),
            "k": bf(np.random.standard_normal((N, T, E)) * g / s),
            "v": bf(np.random.standard_normal((N, T, E)) * 0.0625 * np.sqrt(T))}


def reference(q, k, v):
    q, k, v = f64(q), f64(k), f64(v)
    n_ctx = q.shape[1]
    q = _strided_transpose(q, n_ctx, LOCAL_ATTN_CTX)
    k = _strided_transpose(k, n_ctx, LOCAL_ATTN_CTX)
    v = _strided_transpose(v, n_ctx, LOCAL_ATTN_CTX)
    n_state = q.shape[-1] // HEADS
    scale = 1.0 / np.sqrt(n_state)
    w = mxq(q, 2, "e4m3") @ mxq(k, 2, "e4m3").transpose(0, 2, 1)
    w = w * scale
    p = np.exp(w - w.max(-1, keepdims=True))
    a = (mxq(p, 2, "e4m3") @ mxq(v, 1, "e4m3")) / p.sum(-1, keepdims=True)
    n, t, e = a.shape
    bT_ctx = n_ctx // LOCAL_ATTN_CTX
    a = a.reshape(n, LOCAL_ATTN_CTX, bT_ctx, e)
    a = np.transpose(a, (0, 2, 1, 3))
    return a.reshape(n, t, e)

@@ -1,0 +1,158 @@
+import math
+from contextlib import ExitStack
+
+import concourse.mybir as mybir
+from concourse.masks import make_identity
+
+F32 = mybir.dt.float32
+BF16 = mybir.dt.bfloat16
+U32 = mybir.dt.uint32
+U8 = mybir.dt.uint8
+FP8X4 = mybir.dt.float8_e4m3fn_x4
+ACT = mybir.ActivationFunctionType
+ALU = mybir.AluOpType
+
+P = 128
+PACK = 4
+T = 512
+E = 512
+HEADS = 16
+TILES = T // P
+HALVES = 2
+SCALE = 1.0 / math.sqrt(E // HEADS)
+
+FLOPS = 2 * 2 * T * T * E
+
+
+def tile_sparseattention_s_kernel(tc, q, k, v, out):
+    nc = tc.nc
+    q_rows = q.flatten_outer_dims().rearrange("(b l) f -> l b f", l=P)
+    k_rows = k.flatten_outer_dims().rearrange("(b l) f -> l b f", l=P)
+    v_rows = v.flatten_outer_dims().rearrange("(b l) f -> l b f", l=P)
+    out_rows = out.flatten_outer_dims().rearrange("(b l) f -> l b f", l=P)
+
+    with ExitStack() as ctx:
+        keep = ctx.enter_context(tc.tile_pool(name="keep", bufs=1))
+        work = ctx.enter_context(tc.tile_pool(name="work", bufs=TILES))
+        psum = ctx.enter_context(tc.psum_pool(name="psum", bufs=4))
+
+        k_sb = [keep.tile([P, E], BF16, name="k_sb%d" % b) for b in range(TILES)]
+        q_sb = [keep.tile([P, E], BF16, name="q_sb%d" % b) for b in range(TILES)]
+        v_sb = keep.tile([P, PACK, E], BF16)
+        for b in range(TILES):
+            nc.sync.dma_start(out=k_sb[b][:], in_=k_rows[:, b, :])
+        for b in range(TILES):
+            nc.sync.dma_start(out=q_sb[b][:], in_=q_rows[:, b, :])
+        nc.sync.dma_start(out=v_sb[:], in_=v_rows)
+
+        ident_f32 = keep.tile([P, P], F32)
+        make_identity(nc, ident_f32[:])
+        ident_bf16 = keep.tile([P, P], BF16)
+        make_identity(nc, ident_bf16[:])
+
+        zero = keep.tile([P, 1], F32)
+        one = keep.tile([P, 1], F32)
+        nc.vector.memset(zero[:], 0.0)
+        nc.scalar.activation(out=one[:], in_=zero[:], func=ACT.Exp)
+
+        k_grouped = keep.tile([P, T * PACK], BF16, align_bytes=64)
+        k_codes = keep.tile([P, T], U32, align_bytes=64)
+        k_scales = keep.tile([P, T], U8, align_bytes=64)
+        q_grouped = keep.tile([P, T * PACK], BF16, align_bytes=64)
+        q_codes = keep.tile([P, T], U32, align_bytes=64)
+        q_scales = keep.tile([P, T], U8, align_bytes=64)
+        v_grouped = keep.tile([P, E, PACK], BF16, align_bytes=64)
+        v_codes = keep.tile([P, E], U32, align_bytes=64)
+        v_scales = keep.tile([P, E], U8, align_bytes=64)
+        e_codes = keep.tile([P, T], U32, align_bytes=64)
+        e_scales = keep.tile([P, T], U8, align_bytes=64)
+
+        def quantise_along_features(x_sb, b, grouped, codes, scales):
+            words = x_sb[:].bitcast(F32)
+            xt = psum.tile([P, HALVES, P], F32, tag="transposed")
+            for u in range(HALVES):
+                nc.tensor.transpose(xt[:, u, :], words[:, u * P : (u + 1) * P], ident_f32[:])
+            dst = grouped[:].bitcast(F32)[:, b * P * HALVES : (b + 1) * P * HALVES]
+            dst = dst.rearrange("p (t u) -> p t u", u=HALVES)
+            src = xt[:].rearrange("p u t -> p t u")
+            if b % 2 == 0:
+                nc.vector.tensor_copy(out=dst, in_=src)
+            else:
+                nc.scalar.copy(out=dst, in_=src)
+            cols = slice(b * P, (b + 1) * P)
+            nc.vector.quantize_mx(
+                out=codes[:, cols].bitcast(FP8X4),
+                scales=scales[:, cols],
+                in_=grouped[:, b * P * PACK : (b + 1) * P * PACK],
+            )
+
+        for b in range(TILES):
+            quantise_along_features(k_sb[b], b, k_grouped, k_codes, k_scales)
+        for b in range(TILES):
+            quantise_along_features(q_sb[b], b, q_grouped, q_codes, q_scales)
+
+        e_tiles = []
+        inv_sums = []
+        for i in range(TILES):
+            cols = slice(i * P, (i + 1) * P)
+            s = psum.tile([P, T], F32, tag="product")
+            nc.tensor.matmul_mx(
+                out=s[:],
+                lhsT=q_codes[:, cols].bitcast(FP8X4),
+                lhsT_scale=q_scales[:, cols],
+                rhs=k_codes[:].bitcast(FP8X4),
+                rhs_scale=k_scales[:],
+                start=True,
+                stop=True,
+            )
+            neg_max = work.tile([P, 1], F32)
+            nc.vector.tensor_reduce(
+                out=neg_max[:], in_=s[:], axis=mybir.AxisListType.X, op=ALU.max, negate=True
+            )
+            bias = work.tile([P, 1], F32)
+            nc.scalar.mul(bias[:], neg_max[:], SCALE)
+            e = work.tile([P, T], BF16)
+            row_sum = work.tile([P, 1], F32)
+            nc.scalar.activation(
+                out=e[:], in_=s[:], func=ACT.Exp, bias=bias[:], scale=SCALE, accum_out=row_sum[:]
+            )
+            inv_sum = work.tile([P, 1], F32)
+            nc.vector.reciprocal(inv_sum[:], row_sum[:])
+            e_tiles.append(e)
+            inv_sums.append(inv_sum)
+
+        nc.vector.tensor_copy(out=v_grouped[:], in_=v_sb[:].rearrange("l b f -> l f b"))
+        nc.vector.quantize_mx(
+            out=v_codes[:].bitcast(FP8X4),
+            scales=v_scales[:],
+            in_=v_grouped[:].rearrange("l f b -> l (f b)"),
+        )
+
+        for i in range(TILES):
+            cols = slice(i * P, (i + 1) * P)
+            et = psum.tile([P, PACK, P], BF16, tag="transposed")
+            for b in range(PACK):
+                nc.tensor.transpose(et[:, b, :], e_tiles[i][:, b * P : (b + 1) * P], ident_bf16[:])
+            e_grouped = work.tile([P, P, PACK], BF16, align_bytes=64)
+            if i % 2 == 0:
+                nc.vector.tensor_copy(out=e_grouped[:], in_=et[:].rearrange("l b t -> l t b"))
+            else:
+                nc.scalar.copy(out=e_grouped[:], in_=et[:].rearrange("l b t -> l t b"))
+            nc.vector.quantize_mx(
+                out=e_codes[:, cols].bitcast(FP8X4),
+                scales=e_scales[:, cols],
+                in_=e_grouped[:].rearrange("l t b -> l (t b)"),
+            )
+            o = psum.tile([P, E], F32, tag="product")
+            nc.tensor.matmul_mx(
+                out=o[:],
+                lhsT=e_codes[:, cols].bitcast(FP8X4),
+                lhsT_scale=e_scales[:, cols],
+                rhs=v_codes[:].bitcast(FP8X4),
+                rhs_scale=v_scales[:],
+                start=True,
+                stop=True,
+            )
+            o_sb = work.tile([P, E], F32)
+            nc.scalar.activation(out=o_sb[:], in_=o[:], func=ACT.Copy, scale=inv_sums[i][:])
+            nc.sync.dma_start(out=out_rows[:, i, :], in_=o_sb[:])

@@ -18,7 +18,10 @@ T = 512
 E = 512
 HEADS = 16
 TILES = T // P
-HALVES = 2
+WORD_HALVES = 2
+OUT_HALVES = 2
+HALF = E // OUT_HALVES
+PSUM_BANKS = 8
 SCALE = 1.0 / math.sqrt(E // HEADS)
 
 FLOPS = 2 * 2 * T * T * E
@@ -34,7 +37,8 @@ def tile_sparseattention_s_kernel(tc, q, k, v, out):
     with ExitStack() as ctx:
         keep = ctx.enter_context(tc.tile_pool(name="keep", bufs=1))
         work = ctx.enter_context(tc.tile_pool(name="work", bufs=TILES))
-        psum = ctx.enter_context(tc.psum_pool(name="psum", bufs=4))
+        psum = ctx.enter_context(tc.psum_pool(name="psum", bufs=PSUM_BANKS))
+        ctx.enter_context(tc.manual_schedule())
 
         k_sb = [keep.tile([P, E], BF16, name="k_sb%d" % b) for b in range(TILES)]
         q_sb = [keep.tile([P, E], BF16, name="q_sb%d" % b) for b in range(TILES)]
@@ -67,18 +71,23 @@ def tile_sparseattention_s_kernel(tc, q, k, v, out):
         e_codes = keep.tile([P, T], U32, align_bytes=64)
         e_scales = keep.tile([P, T], U8, align_bytes=64)
 
-        def quantise_along_features(x_sb, b, grouped, codes, scales):
-            words = x_sb[:].bitcast(F32)
-            xt = psum.tile([P, HALVES, P], F32, tag="transposed")
-            for u in range(HALVES):
-                nc.tensor.transpose(xt[:, u, :], words[:, u * P : (u + 1) * P], ident_f32[:])
-            dst = grouped[:].bitcast(F32)[:, b * P * HALVES : (b + 1) * P * HALVES]
-            dst = dst.rearrange("p (t u) -> p t u", u=HALVES)
-            src = xt[:].rearrange("p u t -> p t u")
-            if b % 2 == 0:
+        def copy_out_of_psum(n, dst, src):
+            if n % 2 == 0:
                 nc.vector.tensor_copy(out=dst, in_=src)
             else:
                 nc.scalar.copy(out=dst, in_=src)
+
+        def features_to_partitions(n, x_sb, b, grouped):
+            words = x_sb[:].bitcast(F32)
+            xt = psum.tile([P, WORD_HALVES, P], F32, tag="bank")
+            for u in range(WORD_HALVES):
+                nc.tensor.transpose(xt[:, u, :], words[:, u * P : (u + 1) * P], ident_f32[:])
+            dst = grouped[:].bitcast(F32)[:, b * P * WORD_HALVES : (b + 1) * P * WORD_HALVES]
+            copy_out_of_psum(
+                n, dst.rearrange("p (t u) -> p t u", u=WORD_HALVES), xt[:].rearrange("p u t -> p t u")
+            )
+
+        def quantise_tile(b, grouped, codes, scales):
             cols = slice(b * P, (b + 1) * P)
             nc.vector.quantize_mx(
                 out=codes[:, cols].bitcast(FP8X4),
@@ -86,16 +95,19 @@ def tile_sparseattention_s_kernel(tc, q, k, v, out):
                 in_=grouped[:, b * P * PACK : (b + 1) * P * PACK],
             )
 
-        for b in range(TILES):
-            quantise_along_features(k_sb[b], b, k_grouped, k_codes, k_scales)
-        for b in range(TILES):
-            quantise_along_features(q_sb[b], b, q_grouped, q_codes, q_scales)
+        landed = [(k_sb[b], b, k_grouped, k_codes, k_scales) for b in range(TILES)]
+        landed += [(q_sb[b], b, q_grouped, q_codes, q_scales) for b in range(TILES)]
+        for n, (x_sb, b, grouped, codes, scales) in enumerate(landed):
+            features_to_partitions(n, x_sb, b, grouped)
+            if n > 0:
+                quantise_tile(*landed[n - 1][1:])
+        quantise_tile(*landed[-1][1:])
 
         e_tiles = []
-        inv_sums = []
+        row_sums = []
         for i in range(TILES):
             cols = slice(i * P, (i + 1) * P)
-            s = psum.tile([P, T], F32, tag="product")
+            s = psum.tile([P, T], F32, tag="bank")
             nc.tensor.matmul_mx(
                 out=s[:],
                 lhsT=q_codes[:, cols].bitcast(FP8X4),
@@ -105,54 +117,76 @@ def tile_sparseattention_s_kernel(tc, q, k, v, out):
                 start=True,
                 stop=True,
             )
-            neg_max = work.tile([P, 1], F32)
-            nc.vector.tensor_reduce(
-                out=neg_max[:], in_=s[:], axis=mybir.AxisListType.X, op=ALU.max, negate=True
-            )
+            scaled = work.tile([P, T], F32)
             bias = work.tile([P, 1], F32)
-            nc.scalar.mul(bias[:], neg_max[:], SCALE)
+            nc.vector.tensor_scalar(
+                out=scaled[:],
+                in0=s[:],
+                scalar1=-SCALE,
+                scalar2=None,
+                op0=ALU.mult,
+                op1=ALU.min,
+                accum_out=bias[:],
+            )
             e = work.tile([P, T], BF16)
             row_sum = work.tile([P, 1], F32)
             nc.scalar.activation(
                 out=e[:], in_=s[:], func=ACT.Exp, bias=bias[:], scale=SCALE, accum_out=row_sum[:]
             )
-            inv_sum = work.tile([P, 1], F32)
-            nc.vector.reciprocal(inv_sum[:], row_sum[:])
             e_tiles.append(e)
-            inv_sums.append(inv_sum)
+            row_sums.append(row_sum)
 
-        nc.vector.tensor_copy(out=v_grouped[:], in_=v_sb[:].rearrange("l b f -> l f b"))
+        nc.vector.tensor_copy(
+            out=v_grouped[:].rearrange("l (c i) b -> l c b i", i=4),
+            in_=v_sb[:].rearrange("l b (c i) -> l c b i", i=4),
+        )
         nc.vector.quantize_mx(
             out=v_codes[:].bitcast(FP8X4),
             scales=v_scales[:],
             in_=v_grouped[:].rearrange("l f b -> l (f b)"),
         )
 
+        e_grouped_tiles = []
         for i in range(TILES):
-            cols = slice(i * P, (i + 1) * P)
-            et = psum.tile([P, PACK, P], BF16, tag="transposed")
+            et = psum.tile([P, PACK, P], BF16, tag="bank")
             for b in range(PACK):
                 nc.tensor.transpose(et[:, b, :], e_tiles[i][:, b * P : (b + 1) * P], ident_bf16[:])
             e_grouped = work.tile([P, P, PACK], BF16, align_bytes=64)
-            if i % 2 == 0:
-                nc.vector.tensor_copy(out=e_grouped[:], in_=et[:].rearrange("l b t -> l t b"))
-            else:
-                nc.scalar.copy(out=e_grouped[:], in_=et[:].rearrange("l b t -> l t b"))
+            nc.scalar.copy(out=e_grouped[:], in_=et[:].rearrange("l b t -> l t b"))
+            e_grouped_tiles.append(e_grouped)
+
+        o_tiles = []
+        inv_sums = []
+        for i in range(TILES):
+            cols = slice(i * P, (i + 1) * P)
+            inv_sum = work.tile([P, 1], F32)
+            nc.vector.reciprocal(inv_sum[:], row_sums[i][:])
+            inv_sums.append(inv_sum)
             nc.vector.quantize_mx(
                 out=e_codes[:, cols].bitcast(FP8X4),
                 scales=e_scales[:, cols],
-                in_=e_grouped[:].rearrange("l t b -> l (t b)"),
+                in_=e_grouped_tiles[i][:].rearrange("l t b -> l (t b)"),
             )
-            o = psum.tile([P, E], F32, tag="product")
-            nc.tensor.matmul_mx(
-                out=o[:],
-                lhsT=e_codes[:, cols].bitcast(FP8X4),
-                lhsT_scale=e_scales[:, cols],
-                rhs=v_codes[:].bitcast(FP8X4),
-                rhs_scale=v_scales[:],
-                start=True,
-                stop=True,
-            )
+            for h in range(OUT_HALVES):
+                feats = slice(h * HALF, (h + 1) * HALF)
+                o = psum.tile([P, HALF], F32, tag="bank")
+                nc.tensor.matmul_mx(
+                    out=o[:],
+                    lhsT=e_codes[:, cols].bitcast(FP8X4),
+                    lhsT_scale=e_scales[:, cols],
+                    rhs=v_codes[:, feats].bitcast(FP8X4),
+                    rhs_scale=v_scales[:, feats],
+                    start=True,
+                    stop=True,
+                )
+                o_tiles.append(o)
+
+        for i in range(TILES):
             o_sb = work.tile([P, E], F32)
-            nc.scalar.activation(out=o_sb[:], in_=o[:], func=ACT.Copy, scale=inv_sums[i][:])
+            nc.vector.tensor_scalar_mul(
+                out=o_sb[:, :HALF], in0=o_tiles[OUT_HALVES * i][:], scalar1=inv_sums[i][:]
+            )
+            nc.scalar.activation(
+                out=o_sb[:, HALF:], in_=o_tiles[OUT_HALVES * i + 1][:], func=ACT.Copy, scale=inv_sums[i][:]
+            )
             nc.sync.dma_start(out=out_rows[:, i, :], in_=o_sb[:])

@@ -14,11 +14,13 @@ ALU = mybir.AluOpType
 
 P = 128
 PACK = 4
+PAIR = 2
 T = 512
 E = 512
 HEADS = 16
 TILES = T // P
-WORD_HALVES = 2
+ROW_WORDS = E // PAIR
+WORD_TILES = ROW_WORDS // P
 OUT_HALVES = 2
 HALF = E // OUT_HALVES
 PSUM_BANKS = 8
@@ -49,10 +51,8 @@ def tile_sparseattention_s_kernel(tc, q, k, v, out):
             nc.sync.dma_start(out=q_sb[b][:], in_=q_rows[:, b, :])
         nc.sync.dma_start(out=v_sb[:], in_=v_rows)
 
-        ident_f32 = keep.tile([P, P], F32)
-        make_identity(nc, ident_f32[:])
-        ident_bf16 = keep.tile([P, P], BF16)
-        make_identity(nc, ident_bf16[:])
+        ident = keep.tile([P, P], F32)
+        make_identity(nc, ident[:])
 
         zero = keep.tile([P, 1], F32)
         one = keep.tile([P, 1], F32)
@@ -65,46 +65,68 @@ def tile_sparseattention_s_kernel(tc, q, k, v, out):
         q_grouped = keep.tile([P, T * PACK], BF16, align_bytes=64)
         q_codes = keep.tile([P, T], U32, align_bytes=64)
         q_scales = keep.tile([P, T], U8, align_bytes=64)
+        e_grouped = keep.tile([P, T * PACK], BF16, align_bytes=64)
+        e_codes = keep.tile([P, T], U32, align_bytes=64)
+        e_scales = keep.tile([P, T], U8, align_bytes=64)
         v_grouped = keep.tile([P, E, PACK], BF16, align_bytes=64)
         v_codes = keep.tile([P, E], U32, align_bytes=64)
         v_scales = keep.tile([P, E], U8, align_bytes=64)
-        e_codes = keep.tile([P, T], U32, align_bytes=64)
-        e_scales = keep.tile([P, T], U8, align_bytes=64)
 
-        def copy_out_of_psum(n, dst, src):
-            if n % 2 == 0:
-                nc.vector.tensor_copy(out=dst, in_=src)
-            else:
-                nc.scalar.copy(out=dst, in_=src)
-
-        def features_to_partitions(n, x_sb, b, grouped):
-            words = x_sb[:].bitcast(F32)
-            xt = psum.tile([P, WORD_HALVES, P], F32, tag="bank")
-            for u in range(WORD_HALVES):
-                nc.tensor.transpose(xt[:, u, :], words[:, u * P : (u + 1) * P], ident_f32[:])
-            dst = grouped[:].bitcast(F32)[:, b * P * WORD_HALVES : (b + 1) * P * WORD_HALVES]
-            copy_out_of_psum(
-                n, dst.rearrange("p (t u) -> p t u", u=WORD_HALVES), xt[:].rearrange("p u t -> p t u")
-            )
-
-        def quantise_tile(b, grouped, codes, scales):
-            cols = slice(b * P, (b + 1) * P)
+        def quantise(grouped, codes, scales, first_col, n_cols):
             nc.vector.quantize_mx(
-                out=codes[:, cols].bitcast(FP8X4),
-                scales=scales[:, cols],
-                in_=grouped[:, b * P * PACK : (b + 1) * P * PACK],
+                out=codes[:, first_col : first_col + n_cols].bitcast(FP8X4),
+                scales=scales[:, first_col : first_col + n_cols],
+                in_=grouped[:, first_col * PACK : (first_col + n_cols) * PACK],
             )
 
-        landed = [(k_sb[b], b, k_grouped, k_codes, k_scales) for b in range(TILES)]
-        landed += [(q_sb[b], b, q_grouped, q_codes, q_scales) for b in range(TILES)]
-        for n, (x_sb, b, grouped, codes, scales) in enumerate(landed):
-            features_to_partitions(n, x_sb, b, grouped)
-            if n > 0:
-                quantise_tile(*landed[n - 1][1:])
-        quantise_tile(*landed[-1][1:])
+        def transpose_words(bank_part, rows):
+            words = rows.bitcast(F32)
+            for w in range(WORD_TILES):
+                nc.tensor.transpose(bank_part[:, w, :], words[:, w * P : (w + 1) * P], ident[:])
+
+        def rows_to_columns(copy, rows, grouped, i):
+            bank = psum.tile([P, WORD_TILES, P], F32, tag="bank")
+            transpose_words(bank, rows)
+            dst = grouped[:].bitcast(F32)[:, i * P * WORD_TILES : (i + 1) * P * WORD_TILES]
+            copy(
+                out=dst.rearrange("p (r w) -> p r w", w=WORD_TILES),
+                in_=bank[:].rearrange("p w r -> p r w"),
+            )
+
+        def two_key_tiles_to_columns(copy, u):
+            bank = psum.tile([P, PAIR, WORD_TILES, P], F32, tag="bank")
+            for c in range(PAIR):
+                transpose_words(bank[:, c], k_sb[PAIR * u + c][:])
+            dst = k_grouped[:].bitcast(F32)[:, u * PAIR * ROW_WORDS : (u + 1) * PAIR * ROW_WORDS]
+            copy(
+                out=dst.rearrange("p (l c w) -> p l c w", c=PAIR, w=WORD_TILES),
+                in_=bank[:].rearrange("p c w l -> p l c w"),
+            )
+
+        two_key_tiles_to_columns(nc.vector.tensor_copy, 0)
+        quantise(k_grouped, k_codes, k_scales, 0, PAIR * P)
+        two_key_tiles_to_columns(nc.scalar.copy, 1)
+        rows_to_columns(nc.vector.tensor_copy, q_sb[0][:], q_grouped, 0)
+        quantise(k_grouped, k_codes, k_scales, PAIR * P, PAIR * P)
+        quantise(q_grouped, q_codes, q_scales, 0, P)
+        rows_to_columns(nc.scalar.copy, q_sb[1][:], q_grouped, 1)
+        rows_to_columns(nc.vector.tensor_copy, q_sb[2][:], q_grouped, 2)
+        quantise(q_grouped, q_codes, q_scales, P, P)
+        rows_to_columns(nc.scalar.copy, q_sb[3][:], q_grouped, 3)
+        quantise(q_grouped, q_codes, q_scales, 2 * P, P)
+        quantise(q_grouped, q_codes, q_scales, 3 * P, P)
+
+        nc.gpsimd.tensor_scalar(
+            out=v_grouped[:],
+            in0=v_sb[:].rearrange("l b f -> l f b"),
+            scalar1=1.0,
+            scalar2=0.0,
+            op0=ALU.mult,
+            op1=ALU.add,
+        )
 
         e_tiles = []
-        row_sums = []
+        row_sums = keep.tile([P, TILES], F32)
         for i in range(TILES):
             cols = slice(i * P, (i + 1) * P)
             s = psum.tile([P, T], F32, tag="bank")
@@ -129,44 +151,35 @@ def tile_sparseattention_s_kernel(tc, q, k, v, out):
                 accum_out=bias[:],
             )
             e = work.tile([P, T], BF16)
-            row_sum = work.tile([P, 1], F32)
             nc.scalar.activation(
-                out=e[:], in_=s[:], func=ACT.Exp, bias=bias[:], scale=SCALE, accum_out=row_sum[:]
+                out=e[:],
+                in_=s[:],
+                func=ACT.Exp,
+                bias=bias[:],
+                scale=SCALE,
+                accum_out=row_sums[:, i : i + 1],
             )
             e_tiles.append(e)
-            row_sums.append(row_sum)
 
-        nc.vector.tensor_copy(
-            out=v_grouped[:].rearrange("l (c i) b -> l c b i", i=4),
-            in_=v_sb[:].rearrange("l b (c i) -> l c b i", i=4),
-        )
+        rows_to_columns(nc.vector.tensor_copy, e_tiles[0][:], e_grouped, 0)
+        rows_to_columns(nc.vector.tensor_copy, e_tiles[1][:], e_grouped, 1)
+        rows_to_columns(nc.scalar.copy, e_tiles[2][:], e_grouped, 2)
+        rows_to_columns(nc.scalar.copy, e_tiles[3][:], e_grouped, 3)
+
+        quantise(e_grouped, e_codes, e_scales, 0, P)
         nc.vector.quantize_mx(
             out=v_codes[:].bitcast(FP8X4),
             scales=v_scales[:],
             in_=v_grouped[:].rearrange("l f b -> l (f b)"),
         )
+        inv_sums = keep.tile([P, TILES], F32)
+        nc.vector.reciprocal(inv_sums[:], row_sums[:])
 
-        e_grouped_tiles = []
-        for i in range(TILES):
-            et = psum.tile([P, PACK, P], BF16, tag="bank")
-            for b in range(PACK):
-                nc.tensor.transpose(et[:, b, :], e_tiles[i][:, b * P : (b + 1) * P], ident_bf16[:])
-            e_grouped = work.tile([P, P, PACK], BF16, align_bytes=64)
-            nc.scalar.copy(out=e_grouped[:], in_=et[:].rearrange("l b t -> l t b"))
-            e_grouped_tiles.append(e_grouped)
-
-        o_tiles = []
-        inv_sums = []
+        o_banks = []
         for i in range(TILES):
             cols = slice(i * P, (i + 1) * P)
-            inv_sum = work.tile([P, 1], F32)
-            nc.vector.reciprocal(inv_sum[:], row_sums[i][:])
-            inv_sums.append(inv_sum)
-            nc.vector.quantize_mx(
-                out=e_codes[:, cols].bitcast(FP8X4),
-                scales=e_scales[:, cols],
-                in_=e_grouped_tiles[i][:].rearrange("l t b -> l (t b)"),
-            )
+            if i > 0:
+                quantise(e_grouped, e_codes, e_scales, i * P, P)
             for h in range(OUT_HALVES):
                 feats = slice(h * HALF, (h + 1) * HALF)
                 o = psum.tile([P, HALF], F32, tag="bank")
@@ -179,14 +192,16 @@ def tile_sparseattention_s_kernel(tc, q, k, v, out):
                     start=True,
                     stop=True,
                 )
-                o_tiles.append(o)
+                o_banks.append(o)
 
         for i in range(TILES):
+            inv_sum = inv_sums[:, i : i + 1]
             o_sb = work.tile([P, E], F32)
             nc.vector.tensor_scalar_mul(
-                out=o_sb[:, :HALF], in0=o_tiles[OUT_HALVES * i][:], scalar1=inv_sums[i][:]
+                out=o_sb[:, :HALF], in0=o_banks[OUT_HALVES * i][:], scalar1=inv_sum
             )
+            nc.sync.dma_start(out=out_rows[:, i, :HALF], in_=o_sb[:, :HALF])
             nc.scalar.activation(
-                out=o_sb[:, HALF:], in_=o_tiles[OUT_HALVES * i + 1][:], func=ACT.Copy, scale=inv_sums[i][:]
+                out=o_sb[:, HALF:], in_=o_banks[OUT_HALVES * i + 1][:], func=ACT.Copy, scale=inv_sum
             )
-            nc.sync.dma_start(out=out_rows[:, i, :], in_=o_sb[:])
+            nc.sync.dma_start(out=out_rows[:, i, HALF:], in_=o_sb[:, HALF:])

@@ -24,6 +24,7 @@ WORD_TILES = ROW_WORDS // P
 OUT_HALVES = 2
 HALF = E // OUT_HALVES
 PSUM_BANKS = 8
+WARM_UP = 4
 SCALE = 1.0 / math.sqrt(E // HEADS)
 
 FLOPS = 2 * 2 * T * T * E
@@ -58,6 +59,12 @@ def tile_sparseattention_s_kernel(tc, q, k, v, out):
         one = keep.tile([P, 1], F32)
         nc.vector.memset(zero[:], 0.0)
         nc.scalar.activation(out=one[:], in_=zero[:], func=ACT.Exp)
+
+        zeros = keep.tile([P, P], F32)
+        nc.vector.memset(zeros[:], 0.0)
+        idle = psum.tile([P, P], F32, tag="bank")
+        for i in range(WARM_UP):
+            nc.tensor.matmul(idle[:], lhsT=zeros[:], rhs=zeros[:], start=True, stop=True)
 
         k_grouped = keep.tile([P, T * PACK], BF16, align_bytes=64)
         k_codes = keep.tile([P, T], U32, align_bytes=64)

@@ -24,7 +24,7 @@ WORD_TILES = ROW_WORDS // P
 OUT_HALVES = 2
 HALF = E // OUT_HALVES
 PSUM_BANKS = 8
-WARM_UP = 4
+WARM_UP = 3
 SCALE = 1.0 / math.sqrt(E // HEADS)
 
 FLOPS = 2 * 2 * T * T * E
@@ -55,13 +55,12 @@ def tile_sparseattention_s_kernel(tc, q, k, v, out):
         ident = keep.tile([P, P], F32)
         make_identity(nc, ident[:])
 
-        zero = keep.tile([P, 1], F32)
-        one = keep.tile([P, 1], F32)
-        nc.vector.memset(zero[:], 0.0)
-        nc.scalar.activation(out=one[:], in_=zero[:], func=ACT.Exp)
-
         zeros = keep.tile([P, P], F32)
         nc.vector.memset(zeros[:], 0.0)
+
+        one = keep.tile([P, 1], F32)
+        nc.scalar.activation(out=one[:], in_=zeros[:, 0:1], func=ACT.Exp)
+
         idle = psum.tile([P, P], F32, tag="bank")
         for i in range(WARM_UP):
             nc.tensor.matmul(idle[:], lhsT=zeros[:], rhs=zeros[:], start=True, stop=True)
@@ -100,37 +99,35 @@ def tile_sparseattention_s_kernel(tc, q, k, v, out):
                 in_=bank[:].rearrange("p w r -> p r w"),
             )
 
-        def two_key_tiles_to_columns(copy, u):
-            bank = psum.tile([P, PAIR, WORD_TILES, P], F32, tag="bank")
-            for c in range(PAIR):
-                transpose_words(bank[:, c], k_sb[PAIR * u + c][:])
-            dst = k_grouped[:].bitcast(F32)[:, u * PAIR * ROW_WORDS : (u + 1) * PAIR * ROW_WORDS]
-            copy(
-                out=dst.rearrange("p (l c w) -> p l c w", c=PAIR, w=WORD_TILES),
-                in_=bank[:].rearrange("p c w l -> p l c w"),
+        for b in range(TILES):
+            rows_to_columns(
+                (nc.vector.tensor_copy, nc.scalar.copy)[b % 2], k_sb[b][:], k_grouped, b
+            )
+        for u in range(TILES // PAIR):
+            quantise(k_grouped, k_codes, k_scales, u * PAIR * P, PAIR * P)
+        for i in range(TILES):
+            rows_to_columns(nc.scalar.copy, q_sb[i][:], q_grouped, i)
+            if i < TILES - 1:
+                quantise(q_grouped, q_codes, q_scales, i * P, P)
+
+        for h in range(OUT_HALVES):
+            feats = slice(h * HALF, (h + 1) * HALF)
+            nc.gpsimd.tensor_scalar(
+                out=v_grouped[:, feats, :],
+                in0=v_sb[:, :, feats].rearrange("l b f -> l f b"),
+                scalar1=1.0,
+                scalar2=0.0,
+                op0=ALU.mult,
+                op1=ALU.add,
             )
 
-        two_key_tiles_to_columns(nc.vector.tensor_copy, 0)
-        quantise(k_grouped, k_codes, k_scales, 0, PAIR * P)
-        two_key_tiles_to_columns(nc.scalar.copy, 1)
-        rows_to_columns(nc.vector.tensor_copy, q_sb[0][:], q_grouped, 0)
-        quantise(k_grouped, k_codes, k_scales, PAIR * P, PAIR * P)
-        quantise(q_grouped, q_codes, q_scales, 0, P)
-        rows_to_columns(nc.scalar.copy, q_sb[1][:], q_grouped, 1)
-        rows_to_columns(nc.vector.tensor_copy, q_sb[2][:], q_grouped, 2)
-        quantise(q_grouped, q_codes, q_scales, P, P)
-        rows_to_columns(nc.scalar.copy, q_sb[3][:], q_grouped, 3)
-        quantise(q_grouped, q_codes, q_scales, 2 * P, P)
-        quantise(q_grouped, q_codes, q_scales, 3 * P, P)
-
-        nc.gpsimd.tensor_scalar(
-            out=v_grouped[:],
-            in0=v_sb[:].rearrange("l b f -> l f b"),
-            scalar1=1.0,
-            scalar2=0.0,
-            op0=ALU.mult,
-            op1=ALU.add,
-        )
+        def quantise_v(h):
+            feats = slice(h * HALF, (h + 1) * HALF)
+            nc.vector.quantize_mx(
+                out=v_codes[:, feats].bitcast(FP8X4),
+                scales=v_scales[:, feats],
+                in_=v_grouped[:, feats, :].rearrange("l f b -> l (f b)"),
+            )
 
         e_tiles = []
         row_sums = keep.tile([P, TILES], F32)
@@ -157,10 +154,12 @@ def tile_sparseattention_s_kernel(tc, q, k, v, out):
                 op1=ALU.min,
                 accum_out=bias[:],
             )
+            if i == 0:
+                quantise(q_grouped, q_codes, q_scales, (TILES - 1) * P, P)
             e = work.tile([P, T], BF16)
             nc.scalar.activation(
-                out=e[:],
-                in_=s[:],
+                out=e[:].rearrange("p (u l c) -> p u l c", u=T // (PAIR * P), c=PAIR),
+                in_=s[:].rearrange("p (u c l) -> p u l c", u=T // (PAIR * P), c=PAIR),
                 func=ACT.Exp,
                 bias=bias[:],
                 scale=SCALE,
@@ -168,25 +167,27 @@ def tile_sparseattention_s_kernel(tc, q, k, v, out):
             )
             e_tiles.append(e)
 
+        inv_sums = keep.tile([P, TILES], F32)
+
+        def invert_sums(first, n):
+            nc.vector.reciprocal(inv_sums[:, first : first + n], row_sums[:, first : first + n])
+
+        quantise_v(0)
         rows_to_columns(nc.vector.tensor_copy, e_tiles[0][:], e_grouped, 0)
         rows_to_columns(nc.vector.tensor_copy, e_tiles[1][:], e_grouped, 1)
+        quantise(e_grouped, e_codes, e_scales, 0, P)
+        quantise_v(1)
+        quantise(e_grouped, e_codes, e_scales, P, P)
         rows_to_columns(nc.scalar.copy, e_tiles[2][:], e_grouped, 2)
         rows_to_columns(nc.scalar.copy, e_tiles[3][:], e_grouped, 3)
+        invert_sums(0, 2)
+        invert_sums(2, 2)
 
-        quantise(e_grouped, e_codes, e_scales, 0, P)
-        nc.vector.quantize_mx(
-            out=v_codes[:].bitcast(FP8X4),
-            scales=v_scales[:],
-            in_=v_grouped[:].rearrange("l f b -> l (f b)"),
-        )
-        inv_sums = keep.tile([P, TILES], F32)
-        nc.vector.reciprocal(inv_sums[:], row_sums[:])
-
-        o_banks = []
         for i in range(TILES):
             cols = slice(i * P, (i + 1) * P)
-            if i > 0:
-                quantise(e_grouped, e_codes, e_scales, i * P, P)
+            inv_sum = inv_sums[:, i : i + 1]
+            o_sb = work.tile([P, E], F32)
+            o_banks = []
             for h in range(OUT_HALVES):
                 feats = slice(h * HALF, (h + 1) * HALF)
                 o = psum.tile([P, HALF], F32, tag="bank")
@@ -200,15 +201,11 @@ def tile_sparseattention_s_kernel(tc, q, k, v, out):
                     stop=True,
                 )
                 o_banks.append(o)
-
-        for i in range(TILES):
-            inv_sum = inv_sums[:, i : i + 1]
-            o_sb = work.tile([P, E], F32)
-            nc.vector.tensor_scalar_mul(
-                out=o_sb[:, :HALF], in0=o_banks[OUT_HALVES * i][:], scalar1=inv_sum
-            )
+            nc.vector.tensor_scalar_mul(out=o_sb[:, :HALF], in0=o_banks[0][:], scalar1=inv_sum)
             nc.sync.dma_start(out=out_rows[:, i, :HALF], in_=o_sb[:, :HALF])
             nc.scalar.activation(
-                out=o_sb[:, HALF:], in_=o_banks[OUT_HALVES * i + 1][:], func=ACT.Copy, scale=inv_sum
+                out=o_sb[:, HALF:], in_=o_banks[1][:], func=ACT.Copy, scale=inv_sum
             )
             nc.sync.dma_start(out=out_rows[:, i, HALF:], in_=o_sb[:, HALF:])
+            if i + 2 < TILES:
+                quantise(e_grouped, e_codes, e_scales, (i + 2) * P, P)

@@ -68,13 +68,13 @@ def tile_sparseattention_s_kernel(tc, q, k, v, out):
         k_grouped = keep.tile([P, T * PACK], BF16, align_bytes=64)
         k_codes = keep.tile([P, T], U32, align_bytes=64)
         k_scales = keep.tile([P, T], U8, align_bytes=64)
-        q_grouped = keep.tile([P, T * PACK], BF16, align_bytes=64)
+        q_grouped = keep.tile([P, T * PACK], BF16, align_bytes=64, tag="q_then_v")
         q_codes = keep.tile([P, T], U32, align_bytes=64)
         q_scales = keep.tile([P, T], U8, align_bytes=64)
         e_grouped = keep.tile([P, T * PACK], BF16, align_bytes=64)
         e_codes = keep.tile([P, T], U32, align_bytes=64)
         e_scales = keep.tile([P, T], U8, align_bytes=64)
-        v_grouped = keep.tile([P, E, PACK], BF16, align_bytes=64)
+        v_grouped = keep.tile([P, E, PACK], BF16, align_bytes=64, tag="q_then_v")
         v_codes = keep.tile([P, E], U32, align_bytes=64)
         v_scales = keep.tile([P, E], U8, align_bytes=64)
 
@@ -107,8 +107,7 @@ def tile_sparseattention_s_kernel(tc, q, k, v, out):
             quantise(k_grouped, k_codes, k_scales, u * PAIR * P, PAIR * P)
         for i in range(TILES):
             rows_to_columns(nc.scalar.copy, q_sb[i][:], q_grouped, i)
-            if i < TILES - 1:
-                quantise(q_grouped, q_codes, q_scales, i * P, P)
+            quantise(q_grouped, q_codes, q_scales, i * P, P)
 
         for h in range(OUT_HALVES):
             feats = slice(h * HALF, (h + 1) * HALF)
@@ -154,8 +153,6 @@ def tile_sparseattention_s_kernel(tc, q, k, v, out):
                 op1=ALU.min,
                 accum_out=bias[:],
             )
-            if i == 0:
-                quantise(q_grouped, q_codes, q_scales, (TILES - 1) * P, P)
             e = work.tile([P, T], BF16)
             nc.scalar.activation(
                 out=e[:].rearrange("p (u l c) -> p u l c", u=T // (PAIR * P), c=PAIR),

@@ -169,16 +169,17 @@ def tile_sparseattention_s_kernel(tc, q, k, v, out):
         def invert_sums(first, n):
             nc.vector.reciprocal(inv_sums[:, first : first + n], row_sums[:, first : first + n])
 
-        quantise_v(0)
         rows_to_columns(nc.vector.tensor_copy, e_tiles[0][:], e_grouped, 0)
         rows_to_columns(nc.vector.tensor_copy, e_tiles[1][:], e_grouped, 1)
-        quantise(e_grouped, e_codes, e_scales, 0, P)
-        quantise_v(1)
-        quantise(e_grouped, e_codes, e_scales, P, P)
         rows_to_columns(nc.scalar.copy, e_tiles[2][:], e_grouped, 2)
         rows_to_columns(nc.scalar.copy, e_tiles[3][:], e_grouped, 3)
+        quantise(e_grouped, e_codes, e_scales, 0, P)
+        quantise_v(0)
+        quantise_v(1)
+        quantise(e_grouped, e_codes, e_scales, P, P)
         invert_sums(0, 2)
         invert_sums(2, 2)
+        quantise(e_grouped, e_codes, e_scales, 2 * P, P)
 
         for i in range(TILES):
             cols = slice(i * P, (i + 1) * P)
@@ -204,5 +205,5 @@ def tile_sparseattention_s_kernel(tc, q, k, v, out):
                 out=o_sb[:, HALF:], in_=o_banks[1][:], func=ACT.Copy, scale=inv_sum
             )
             nc.sync.dma_start(out=out_rows[:, i, HALF:], in_=o_sb[:, HALF:])
-            if i + 2 < TILES:
-                quantise(e_grouped, e_codes, e_scales, (i + 2) * P, P)
+            if i == 0:
+                quantise(e_grouped, e_codes, e_scales, (TILES - 1) * P, P)

@@ -23,8 +23,10 @@ ROW_WORDS = E // PAIR
 WORD_TILES = ROW_WORDS // P
 OUT_HALVES = 2
 HALF = E // OUT_HALVES
+SCALAR_FEATS = 128
 PSUM_BANKS = 8
 WARM_UP = 3
+GPSIMD_FEATS = ((0, HALF), (HALF, E - HALF - SCALAR_FEATS))
 SCALE = 1.0 / math.sqrt(E // HEADS)
 
 FLOPS = 2 * 2 * T * T * E
@@ -75,6 +77,7 @@ def tile_sparseattention_s_kernel(tc, q, k, v, out):
         e_codes = keep.tile([P, T], U32, align_bytes=64)
         e_scales = keep.tile([P, T], U8, align_bytes=64)
         v_grouped = keep.tile([P, E, PACK], BF16, align_bytes=64, tag="q_then_v")
+        v_grouped_last = keep.tile([P, SCALAR_FEATS, PACK], BF16, align_bytes=64)
         v_codes = keep.tile([P, E], U32, align_bytes=64)
         v_scales = keep.tile([P, E], U8, align_bytes=64)
 
@@ -109,8 +112,8 @@ def tile_sparseattention_s_kernel(tc, q, k, v, out):
             rows_to_columns(nc.scalar.copy, q_sb[i][:], q_grouped, i)
             quantise(q_grouped, q_codes, q_scales, i * P, P)
 
-        for h in range(OUT_HALVES):
-            feats = slice(h * HALF, (h + 1) * HALF)
+        for first, n in GPSIMD_FEATS:
+            feats = slice(first, first + n)
             nc.gpsimd.tensor_scalar(
                 out=v_grouped[:, feats, :],
                 in0=v_sb[:, :, feats].rearrange("l b f -> l f b"),
@@ -119,13 +122,17 @@ def tile_sparseattention_s_kernel(tc, q, k, v, out):
                 op0=ALU.mult,
                 op1=ALU.add,
             )
+        nc.scalar.copy(
+            out=v_grouped_last[:],
+            in_=v_sb[:, :, E - SCALAR_FEATS :].rearrange("l b f -> l f b"),
+        )
 
-        def quantise_v(h):
-            feats = slice(h * HALF, (h + 1) * HALF)
+        def quantise_v(first, n, grouped):
+            feats = slice(first, first + n)
             nc.vector.quantize_mx(
                 out=v_codes[:, feats].bitcast(FP8X4),
                 scales=v_scales[:, feats],
-                in_=v_grouped[:, feats, :].rearrange("l f b -> l (f b)"),
+                in_=grouped.rearrange("l f b -> l (f b)"),
             )
 
         e_tiles = []
@@ -169,17 +176,18 @@ def tile_sparseattention_s_kernel(tc, q, k, v, out):
         def invert_sums(first, n):
             nc.vector.reciprocal(inv_sums[:, first : first + n], row_sums[:, first : first + n])
 
+        (first_half, rest) = GPSIMD_FEATS
         rows_to_columns(nc.vector.tensor_copy, e_tiles[0][:], e_grouped, 0)
+        quantise_v(*first_half, v_grouped[:, :HALF, :])
+        quantise(e_grouped, e_codes, e_scales, 0, P)
         rows_to_columns(nc.vector.tensor_copy, e_tiles[1][:], e_grouped, 1)
+        quantise_v(*rest, v_grouped[:, HALF : E - SCALAR_FEATS, :])
+        quantise_v(E - SCALAR_FEATS, SCALAR_FEATS, v_grouped_last[:])
         rows_to_columns(nc.scalar.copy, e_tiles[2][:], e_grouped, 2)
         rows_to_columns(nc.scalar.copy, e_tiles[3][:], e_grouped, 3)
-        quantise(e_grouped, e_codes, e_scales, 0, P)
-        quantise_v(0)
-        quantise_v(1)
-        quantise(e_grouped, e_codes, e_scales, P, P)
         invert_sums(0, 2)
+        quantise(e_grouped, e_codes, e_scales, P, P)
         invert_sums(2, 2)
-        quantise(e_grouped, e_codes, e_scales, 2 * P, P)
 
         for i in range(TILES):
             cols = slice(i * P, (i + 1) * P)
@@ -199,11 +207,16 @@ def tile_sparseattention_s_kernel(tc, q, k, v, out):
                     stop=True,
                 )
                 o_banks.append(o)
-            nc.vector.tensor_scalar_mul(out=o_sb[:, :HALF], in0=o_banks[0][:], scalar1=inv_sum)
-            nc.sync.dma_start(out=out_rows[:, i, :HALF], in_=o_sb[:, :HALF])
-            nc.scalar.activation(
-                out=o_sb[:, HALF:], in_=o_banks[1][:], func=ACT.Copy, scale=inv_sum
-            )
-            nc.sync.dma_start(out=out_rows[:, i, HALF:], in_=o_sb[:, HALF:])
-            if i == 0:
-                quantise(e_grouped, e_codes, e_scales, (TILES - 1) * P, P)
+            for h in range(OUT_HALVES):
+                feats = slice(h * HALF, (h + 1) * HALF)
+                if h == 0 and i < TILES - 1:
+                    nc.vector.tensor_scalar_mul(
+                        out=o_sb[:, feats], in0=o_banks[h][:], scalar1=inv_sum
+                    )
+                else:
+                    nc.scalar.activation(
+                        out=o_sb[:, feats], in_=o_banks[h][:], func=ACT.Copy, scale=inv_sum
+                    )
+                nc.sync.dma_start(out=out_rows[:, i, feats], in_=o_sb[:, feats])
+            if i + 2 < TILES:
+                quantise(e_grouped, e_codes, e_scales, (i + 2) * P, P)

@@ -42,7 +42,8 @@ def tile_sparseattention_s_kernel(tc, q, k, v, out):
     with ExitStack() as ctx:
         keep = ctx.enter_context(tc.tile_pool(name="keep", bufs=1))
         work = ctx.enter_context(tc.tile_pool(name="work", bufs=TILES))
-        psum = ctx.enter_context(tc.psum_pool(name="psum", bufs=PSUM_BANKS))
+        idle_psum = ctx.enter_context(tc.psum_pool(name="idle_psum", bufs=1))
+        psum = ctx.enter_context(tc.psum_pool(name="psum", bufs=PSUM_BANKS - 1))
         ctx.enter_context(tc.manual_schedule())
 
         k_sb = [keep.tile([P, E], BF16, name="k_sb%d" % b) for b in range(TILES)]
@@ -63,9 +64,15 @@ def tile_sparseattention_s_kernel(tc, q, k, v, out):
         one = keep.tile([P, 1], F32)
         nc.scalar.activation(out=one[:], in_=zeros[:, 0:1], func=ACT.Exp)
 
-        idle = psum.tile([P, P], F32, tag="bank")
+        idle = idle_psum.tile([P, P], F32)
+
+        def idle_matmul(n_cols):
+            nc.tensor.matmul(
+                idle[:, :n_cols], lhsT=zeros[:], rhs=zeros[:, :n_cols], start=True, stop=True
+            )
+
         for i in range(WARM_UP):
-            nc.tensor.matmul(idle[:], lhsT=zeros[:], rhs=zeros[:], start=True, stop=True)
+            idle_matmul(P)
 
         k_grouped = keep.tile([P, T * PACK], BF16, align_bytes=64)
         k_codes = keep.tile([P, T], U32, align_bytes=64)
@@ -111,6 +118,7 @@ def tile_sparseattention_s_kernel(tc, q, k, v, out):
         for i in range(TILES):
             rows_to_columns(nc.scalar.copy, q_sb[i][:], q_grouped, i)
             quantise(q_grouped, q_codes, q_scales, i * P, P)
+        idle_matmul(P)
 
         for first, n in GPSIMD_FEATS:
             feats = slice(first, first + n)
@@ -177,13 +185,17 @@ def tile_sparseattention_s_kernel(tc, q, k, v, out):
             nc.vector.reciprocal(inv_sums[:, first : first + n], row_sums[:, first : first + n])
 
         (first_half, rest) = GPSIMD_FEATS
+        idle_matmul(P)
         rows_to_columns(nc.vector.tensor_copy, e_tiles[0][:], e_grouped, 0)
+        idle_matmul(P // 2)
         quantise_v(*first_half, v_grouped[:, :HALF, :])
         quantise(e_grouped, e_codes, e_scales, 0, P)
         rows_to_columns(nc.vector.tensor_copy, e_tiles[1][:], e_grouped, 1)
+        idle_matmul(P // 2)
         quantise_v(*rest, v_grouped[:, HALF : E - SCALAR_FEATS, :])
         quantise_v(E - SCALAR_FEATS, SCALAR_FEATS, v_grouped_last[:])
         rows_to_columns(nc.scalar.copy, e_tiles[2][:], e_grouped, 2)
+        idle_matmul(P // 2)
         rows_to_columns(nc.scalar.copy, e_tiles[3][:], e_grouped, 3)
         invert_sums(0, 2)
         quantise(e_grouped, e_codes, e_scales, P, P)

@@ -19,6 +19,7 @@ T = 512
 E = 512
 HEADS = 16
 TILES = T // P
+STRIDE = 4
 ROW_WORDS = E // PAIR
 WORD_TILES = ROW_WORDS // P
 OUT_HALVES = 2
@@ -34,10 +35,10 @@ FLOPS = 2 * 2 * T * T * E
 
 def tile_sparseattention_s_kernel(tc, q, k, v, out):
     nc = tc.nc
-    q_rows = q.flatten_outer_dims().rearrange("(b l) f -> l b f", l=P)
-    k_rows = k.flatten_outer_dims().rearrange("(b l) f -> l b f", l=P)
-    v_rows = v.flatten_outer_dims().rearrange("(b l) f -> l b f", l=P)
-    out_rows = out.flatten_outer_dims().rearrange("(b l) f -> l b f", l=P)
+    q_rows = q.flatten_outer_dims().rearrange("(p t) f -> p t f", t=TILES)
+    k_rows = k.flatten_outer_dims().rearrange("(p t) f -> p t f", t=TILES)
+    out_rows = out.flatten_outer_dims().rearrange("(p t) f -> p t f", t=TILES)
+    v_rows = v.flatten_outer_dims().rearrange("(b g t) f -> b g (t f)", b=STRIDE, t=PACK)
 
     with ExitStack() as ctx:
         keep = ctx.enter_context(tc.tile_pool(name="keep", bufs=1))
@@ -46,14 +47,17 @@ def tile_sparseattention_s_kernel(tc, q, k, v, out):
         psum = ctx.enter_context(tc.psum_pool(name="psum", bufs=PSUM_BANKS - 1))
         ctx.enter_context(tc.manual_schedule())
 
-        k_sb = [keep.tile([P, E], BF16, name="k_sb%d" % b) for b in range(TILES)]
-        q_sb = [keep.tile([P, E], BF16, name="q_sb%d" % b) for b in range(TILES)]
+        k_sb = keep.tile([P, TILES, E], BF16)
+        q_sb = keep.tile([P, TILES, E], BF16)
         v_sb = keep.tile([P, PACK, E], BF16)
-        for b in range(TILES):
-            nc.sync.dma_start(out=k_sb[b][:], in_=k_rows[:, b, :])
-        for b in range(TILES):
-            nc.sync.dma_start(out=q_sb[b][:], in_=q_rows[:, b, :])
-        nc.sync.dma_start(out=v_sb[:], in_=v_rows)
+        for first, n in ((0, 2), (2, 2)):
+            nc.sync.dma_start(out=k_sb[:, first : first + n], in_=k_rows[:, first : first + n])
+        for first, n in ((0, 1), (1, 1), (2, 2)):
+            nc.sync.dma_start(out=q_sb[:, first : first + n], in_=q_rows[:, first : first + n])
+        for b in range(STRIDE):
+            nc.sync.dma_start(
+                out=v_sb[b:P:STRIDE].rearrange("g t f -> g (t f)"), in_=v_rows[b]
+            )
 
         ident = keep.tile([P, P], F32)
         make_identity(nc, ident[:])
@@ -109,14 +113,21 @@ def tile_sparseattention_s_kernel(tc, q, k, v, out):
                 in_=bank[:].rearrange("p w r -> p r w"),
             )
 
-        for b in range(TILES):
-            rows_to_columns(
-                (nc.vector.tensor_copy, nc.scalar.copy)[b % 2], k_sb[b][:], k_grouped, b
+        def keys_to_columns(copy, t):
+            bank = psum.tile([P, WORD_TILES, P], F32, tag="bank")
+            transpose_words(bank, k_sb[:, t, :])
+            dst = k_grouped[:].bitcast(F32)[:, t * P * WORD_TILES : (t + 1) * P * WORD_TILES]
+            copy(
+                out=dst.rearrange("p (g b w) -> p g b w", b=STRIDE, w=WORD_TILES),
+                in_=bank[:].rearrange("p w (b g) -> p g b w", b=STRIDE),
             )
+
+        for b in range(TILES):
+            keys_to_columns((nc.vector.tensor_copy, nc.scalar.copy)[b % 2], b)
         for u in range(TILES // PAIR):
             quantise(k_grouped, k_codes, k_scales, u * PAIR * P, PAIR * P)
         for i in range(TILES):
-            rows_to_columns(nc.scalar.copy, q_sb[i][:], q_grouped, i)
+            rows_to_columns(nc.scalar.copy, q_sb[:, i, :], q_grouped, i)
             quantise(q_grouped, q_codes, q_scales, i * P, P)
         idle_matmul(P)
 

@@ -75,6 +75,9 @@ def tile_sparseattention_s_kernel(tc, q, k, v, out):
                 idle[:, :n_cols], lhsT=zeros[:], rhs=zeros[:, :n_cols], start=True, stop=True
             )
 
+        words = zeros[:].bitcast(BF16)
+        nc.tensor.matmul(idle[:], lhsT=words[:, :P], rhs=words[:, :P], start=True, stop=True)
+        nc.tensor.matmul(idle[:], lhsT=words[:, :P], rhs=words[:, P:], start=True, stop=True)
         for i in range(WARM_UP):
             idle_matmul(P)
 
@@ -195,51 +198,62 @@ def tile_sparseattention_s_kernel(tc, q, k, v, out):
         def invert_sums(first, n):
             nc.vector.reciprocal(inv_sums[:, first : first + n], row_sums[:, first : first + n])
 
+        o_banks = {}
+
+        def product(i, h):
+            cols = slice(i * P, (i + 1) * P)
+            feats = slice(h * HALF, (h + 1) * HALF)
+            o = psum.tile([P, HALF], F32, tag="bank")
+            nc.tensor.matmul_mx(
+                out=o[:],
+                lhsT=e_codes[:, cols].bitcast(FP8X4),
+                lhsT_scale=e_scales[:, cols],
+                rhs=v_codes[:, feats].bitcast(FP8X4),
+                rhs_scale=v_scales[:, feats],
+                start=True,
+                stop=True,
+            )
+            o_banks[i, h] = o
+
         (first_half, rest) = GPSIMD_FEATS
         idle_matmul(P)
         rows_to_columns(nc.vector.tensor_copy, e_tiles[0][:], e_grouped, 0)
         idle_matmul(P // 2)
         quantise_v(*first_half, v_grouped[:, :HALF, :])
         quantise(e_grouped, e_codes, e_scales, 0, P)
-        rows_to_columns(nc.vector.tensor_copy, e_tiles[1][:], e_grouped, 1)
+        invert_sums(0, 2)
+        rows_to_columns(nc.scalar.copy, e_tiles[1][:], e_grouped, 1)
         idle_matmul(P // 2)
         quantise_v(*rest, v_grouped[:, HALF : E - SCALAR_FEATS, :])
         quantise_v(E - SCALAR_FEATS, SCALAR_FEATS, v_grouped_last[:])
+        quantise(e_grouped, e_codes, e_scales, P, P)
         rows_to_columns(nc.scalar.copy, e_tiles[2][:], e_grouped, 2)
         idle_matmul(P // 2)
+        product(0, 0)
         rows_to_columns(nc.scalar.copy, e_tiles[3][:], e_grouped, 3)
-        invert_sums(0, 2)
-        quantise(e_grouped, e_codes, e_scales, P, P)
-        invert_sums(2, 2)
+        product(0, 1)
 
         for i in range(TILES):
-            cols = slice(i * P, (i + 1) * P)
+            if i > 0:
+                for h in range(OUT_HALVES):
+                    product(i, h)
             inv_sum = inv_sums[:, i : i + 1]
             o_sb = work.tile([P, E], F32)
-            o_banks = []
-            for h in range(OUT_HALVES):
-                feats = slice(h * HALF, (h + 1) * HALF)
-                o = psum.tile([P, HALF], F32, tag="bank")
-                nc.tensor.matmul_mx(
-                    out=o[:],
-                    lhsT=e_codes[:, cols].bitcast(FP8X4),
-                    lhsT_scale=e_scales[:, cols],
-                    rhs=v_codes[:, feats].bitcast(FP8X4),
-                    rhs_scale=v_scales[:, feats],
-                    start=True,
-                    stop=True,
-                )
-                o_banks.append(o)
             for h in range(OUT_HALVES):
                 feats = slice(h * HALF, (h + 1) * HALF)
                 if h == 0 and i < TILES - 1:
                     nc.vector.tensor_scalar_mul(
-                        out=o_sb[:, feats], in0=o_banks[h][:], scalar1=inv_sum
+                        out=o_sb[:, feats], in0=o_banks[i, h][:], scalar1=inv_sum
                     )
                 else:
                     nc.scalar.activation(
-                        out=o_sb[:, feats], in_=o_banks[h][:], func=ACT.Copy, scale=inv_sum
+                        out=o_sb[:, feats], in_=o_banks[i, h][:], func=ACT.Copy, scale=inv_sum
                     )
-                nc.sync.dma_start(out=out_rows[:, i, feats], in_=o_sb[:, feats])
+                if i in (0, TILES - 1):
+                    nc.sync.dma_start(out=out_rows[:, i, feats], in_=o_sb[:, feats])
+            if 0 < i < TILES - 1:
+                nc.sync.dma_start(out=out_rows[:, i, :], in_=o_sb[:])
             if i + 2 < TILES:
                 quantise(e_grouped, e_codes, e_scales, (i + 2) * P, P)
+            if i == 0:
+                invert_sums(2, 2)

@@ -84,14 +84,13 @@ def tile_sparseattention_s_kernel(tc, q, k, v, out):
         k_grouped = keep.tile([P, T * PACK], BF16, align_bytes=64)
         k_codes = keep.tile([P, T], U32, align_bytes=64)
         k_scales = keep.tile([P, T], U8, align_bytes=64)
-        q_grouped = keep.tile([P, T * PACK], BF16, align_bytes=64, tag="q_then_v")
+        q_grouped = keep.tile([P, T * PACK], BF16, align_bytes=64, tag="q_then_gate")
         q_codes = keep.tile([P, T], U32, align_bytes=64)
         q_scales = keep.tile([P, T], U8, align_bytes=64)
         e_grouped = keep.tile([P, T * PACK], BF16, align_bytes=64)
         e_codes = keep.tile([P, T], U32, align_bytes=64)
         e_scales = keep.tile([P, T], U8, align_bytes=64)
-        v_grouped = keep.tile([P, E, PACK], BF16, align_bytes=64, tag="q_then_v")
-        v_grouped_last = keep.tile([P, SCALAR_FEATS, PACK], BF16, align_bytes=64)
+        v_grouped = keep.tile([P, E, PACK], BF16, align_bytes=64)
         v_codes = keep.tile([P, E], U32, align_bytes=64)
         v_scales = keep.tile([P, E], U8, align_bytes=64)
 
@@ -134,6 +133,8 @@ def tile_sparseattention_s_kernel(tc, q, k, v, out):
             quantise(q_grouped, q_codes, q_scales, i * P, P)
         idle_matmul(P)
 
+        gate = keep.tile([P, 1], BF16, align_bytes=64, tag="q_then_gate")
+        nc.gpsimd.memset(gate[:], 0.0)
         for first, n in GPSIMD_FEATS:
             feats = slice(first, first + n)
             nc.gpsimd.tensor_scalar(
@@ -145,16 +146,16 @@ def tile_sparseattention_s_kernel(tc, q, k, v, out):
                 op1=ALU.add,
             )
         nc.scalar.copy(
-            out=v_grouped_last[:],
+            out=v_grouped[:, E - SCALAR_FEATS :, :],
             in_=v_sb[:, :, E - SCALAR_FEATS :].rearrange("l b f -> l f b"),
         )
 
-        def quantise_v(first, n, grouped):
-            feats = slice(first, first + n)
+        def quantise_v(h):
+            feats = slice(h * HALF, (h + 1) * HALF)
             nc.vector.quantize_mx(
                 out=v_codes[:, feats].bitcast(FP8X4),
                 scales=v_scales[:, feats],
-                in_=grouped.rearrange("l f b -> l (f b)"),
+                in_=v_grouped[:, feats, :].rearrange("l f b -> l (f b)"),
             )
 
         e_tiles = []
@@ -215,17 +216,15 @@ def tile_sparseattention_s_kernel(tc, q, k, v, out):
             )
             o_banks[i, h] = o
 
-        (first_half, rest) = GPSIMD_FEATS
         idle_matmul(P)
         rows_to_columns(nc.vector.tensor_copy, e_tiles[0][:], e_grouped, 0)
         idle_matmul(P // 2)
-        quantise_v(*first_half, v_grouped[:, :HALF, :])
+        quantise_v(0)
         quantise(e_grouped, e_codes, e_scales, 0, P)
         invert_sums(0, 2)
         rows_to_columns(nc.scalar.copy, e_tiles[1][:], e_grouped, 1)
         idle_matmul(P // 2)
-        quantise_v(*rest, v_grouped[:, HALF : E - SCALAR_FEATS, :])
-        quantise_v(E - SCALAR_FEATS, SCALAR_FEATS, v_grouped_last[:])
+        quantise_v(1)
         quantise(e_grouped, e_codes, e_scales, P, P)
         rows_to_columns(nc.scalar.copy, e_tiles[2][:], e_grouped, 2)
         idle_matmul(P // 2)

@@ -50,7 +50,7 @@ def tile_sparseattention_s_kernel(tc, q, k, v, out):
         k_sb = keep.tile([P, TILES, E], BF16)
         q_sb = keep.tile([P, TILES, E], BF16)
         v_sb = keep.tile([P, PACK, E], BF16)
-        for first, n in ((0, 2), (2, 2)):
+        for first, n in ((0, 1), (1, 1), (2, 2)):
             nc.sync.dma_start(out=k_sb[:, first : first + n], in_=k_rows[:, first : first + n])
         for first, n in ((0, 1), (1, 1), (2, 2)):
             nc.sync.dma_start(out=q_sb[:, first : first + n], in_=q_rows[:, first : first + n])
@@ -131,7 +131,6 @@ def tile_sparseattention_s_kernel(tc, q, k, v, out):
         for i in range(TILES):
             rows_to_columns(nc.scalar.copy, q_sb[:, i, :], q_grouped, i)
             quantise(q_grouped, q_codes, q_scales, i * P, P)
-        idle_matmul(P)
 
         gate = keep.tile([P, 1], BF16, align_bytes=64, tag="q_then_gate")
         nc.gpsimd.memset(gate[:], 0.0)

@@ -24,7 +24,7 @@ ROW_WORDS = E // PAIR
 WORD_TILES = ROW_WORDS // P
 OUT_HALVES = 2
 HALF = E // OUT_HALVES
-SCALAR_FEATS = 128
+SCALAR_FEATS = 192
 PSUM_BANKS = 8
 WARM_UP = 3
 GPSIMD_FEATS = ((0, HALF), (HALF, E - HALF - SCALAR_FEATS))

@@ -50,7 +50,7 @@ def tile_sparseattention_s_kernel(tc, q, k, v, out):
         k_sb = keep.tile([P, TILES, E], BF16)
         q_sb = keep.tile([P, TILES, E], BF16)
         v_sb = keep.tile([P, PACK, E], BF16)
-        for first, n in ((0, 1), (1, 1), (2, 2)):
+        for first, n in ((0, 1), (1, 1), (2, 1), (3, 1)):
             nc.sync.dma_start(out=k_sb[:, first : first + n], in_=k_rows[:, first : first + n])
         for first, n in ((0, 1), (1, 1), (2, 2)):
             nc.sync.dma_start(out=q_sb[:, first : first + n], in_=q_rows[:, first : first + n])
@@ -215,43 +215,63 @@ def tile_sparseattention_s_kernel(tc, q, k, v, out):
             )
             o_banks[i, h] = o
 
-        idle_matmul(P)
+        def quantise_e(i):
+            quantise(e_grouped, e_codes, e_scales, i * P, P)
+
+        o_sb = []
+        for i in range(TILES):
+            o_tile = work.tile([P, E], F32)
+            o_sb.append(o_tile)
+
+        def divide(i, h, on_vector):
+            feats = slice(h * HALF, (h + 1) * HALF)
+            inv_sum = inv_sums[:, i : i + 1]
+            if on_vector:
+                nc.vector.tensor_scalar_mul(
+                    out=o_sb[i][:, feats], in0=o_banks[i, h][:], scalar1=inv_sum
+                )
+            else:
+                nc.scalar.activation(
+                    out=o_sb[i][:, feats], in_=o_banks[i, h][:], func=ACT.Copy, scale=inv_sum
+                )
+
+        def store(i, feats):
+            nc.sync.dma_start(out=out_rows[:, i, feats], in_=o_sb[i][:, feats])
+
+        idle_matmul(128)
         rows_to_columns(nc.vector.tensor_copy, e_tiles[0][:], e_grouped, 0)
-        idle_matmul(P // 2)
+        idle_matmul(64)
         quantise_v(0)
-        quantise(e_grouped, e_codes, e_scales, 0, P)
+        quantise_e(0)
         invert_sums(0, 2)
         rows_to_columns(nc.scalar.copy, e_tiles[1][:], e_grouped, 1)
-        idle_matmul(P // 2)
+        idle_matmul(64)
         quantise_v(1)
-        quantise(e_grouped, e_codes, e_scales, P, P)
+        quantise_e(1)
         rows_to_columns(nc.scalar.copy, e_tiles[2][:], e_grouped, 2)
-        idle_matmul(P // 2)
+        idle_matmul(64)
         product(0, 0)
         rows_to_columns(nc.scalar.copy, e_tiles[3][:], e_grouped, 3)
         product(0, 1)
-
-        for i in range(TILES):
-            if i > 0:
-                for h in range(OUT_HALVES):
-                    product(i, h)
-            inv_sum = inv_sums[:, i : i + 1]
-            o_sb = work.tile([P, E], F32)
-            for h in range(OUT_HALVES):
-                feats = slice(h * HALF, (h + 1) * HALF)
-                if h == 0 and i < TILES - 1:
-                    nc.vector.tensor_scalar_mul(
-                        out=o_sb[:, feats], in0=o_banks[i, h][:], scalar1=inv_sum
-                    )
-                else:
-                    nc.scalar.activation(
-                        out=o_sb[:, feats], in_=o_banks[i, h][:], func=ACT.Copy, scale=inv_sum
-                    )
-                if i in (0, TILES - 1):
-                    nc.sync.dma_start(out=out_rows[:, i, feats], in_=o_sb[:, feats])
-            if 0 < i < TILES - 1:
-                nc.sync.dma_start(out=out_rows[:, i, :], in_=o_sb[:])
-            if i + 2 < TILES:
-                quantise(e_grouped, e_codes, e_scales, (i + 2) * P, P)
-            if i == 0:
-                invert_sums(2, 2)
+        divide(0, 0, True)
+        store(0, slice(0, HALF))
+        divide(0, 1, False)
+        store(0, slice(HALF, E))
+        quantise_e(2)
+        invert_sums(2, 2)
+        product(1, 0)
+        product(1, 1)
+        divide(1, 0, True)
+        divide(1, 1, False)
+        store(1, slice(0, E))
+        quantise_e(3)
+        product(2, 0)
+        product(2, 1)
+        divide(2, 0, True)
+        divide(2, 1, False)
+        store(2, slice(0, E))
+        product(3, 0)
+        product(3, 1)
+        divide(3, 0, True)
+        divide(3, 1, False)
+        store(3, slice(0, E))

@@ -149,8 +149,8 @@ def tile_sparseattention_s_kernel(tc, q, k, v, out):
             in_=v_sb[:, :, E - SCALAR_FEATS :].rearrange("l b f -> l f b"),
         )
 
-        def quantise_v(h):
-            feats = slice(h * HALF, (h + 1) * HALF)
+        def quantise_v(first, n):
+            feats = slice(first, first + n)
             nc.vector.quantize_mx(
                 out=v_codes[:, feats].bitcast(FP8X4),
                 scales=v_scales[:, feats],
@@ -200,12 +200,12 @@ def tile_sparseattention_s_kernel(tc, q, k, v, out):
 
         o_banks = {}
 
-        def product(i, h):
+        def product(i, first, n):
             cols = slice(i * P, (i + 1) * P)
-            feats = slice(h * HALF, (h + 1) * HALF)
+            feats = slice(first, first + n)
             o = psum.tile([P, HALF], F32, tag="bank")
             nc.tensor.matmul_mx(
-                out=o[:],
+                out=o[:, :n],
                 lhsT=e_codes[:, cols].bitcast(FP8X4),
                 lhsT_scale=e_scales[:, cols],
                 rhs=v_codes[:, feats].bitcast(FP8X4),
@@ -213,7 +213,7 @@ def tile_sparseattention_s_kernel(tc, q, k, v, out):
                 start=True,
                 stop=True,
             )
-            o_banks[i, h] = o
+            o_banks[i, first] = o
 
         def quantise_e(i):
             quantise(e_grouped, e_codes, e_scales, i * P, P)
@@ -223,55 +223,62 @@ def tile_sparseattention_s_kernel(tc, q, k, v, out):
             o_tile = work.tile([P, E], F32)
             o_sb.append(o_tile)
 
-        def divide(i, h, on_vector):
-            feats = slice(h * HALF, (h + 1) * HALF)
+        def divide(engine, i, first, n):
+            out_cols = o_sb[i][:, first : first + n]
             inv_sum = inv_sums[:, i : i + 1]
-            if on_vector:
-                nc.vector.tensor_scalar_mul(
-                    out=o_sb[i][:, feats], in0=o_banks[i, h][:], scalar1=inv_sum
+            if engine == "vector":
+                nc.vector.tensor_tensor(
+                    out=out_cols,
+                    in0=o_banks[i, first][:, :n],
+                    in1=inv_sum.to_broadcast([P, n]),
+                    op=ALU.mult,
                 )
             else:
                 nc.scalar.activation(
-                    out=o_sb[i][:, feats], in_=o_banks[i, h][:], func=ACT.Copy, scale=inv_sum
+                    out=out_cols, in_=o_banks[i, first][:, :n], func=ACT.Copy, scale=inv_sum
                 )
 
-        def store(i, feats):
+        def store(i, first, n):
+            feats = slice(first, first + n)
             nc.sync.dma_start(out=out_rows[:, i, feats], in_=o_sb[i][:, feats])
 
         idle_matmul(128)
         rows_to_columns(nc.vector.tensor_copy, e_tiles[0][:], e_grouped, 0)
         idle_matmul(64)
-        quantise_v(0)
+        quantise_v(0, 128)
         quantise_e(0)
         invert_sums(0, 2)
         rows_to_columns(nc.scalar.copy, e_tiles[1][:], e_grouped, 1)
         idle_matmul(64)
-        quantise_v(1)
+        quantise_v(128, 128)
+        quantise_v(256, 256)
         quantise_e(1)
         rows_to_columns(nc.scalar.copy, e_tiles[2][:], e_grouped, 2)
         idle_matmul(64)
-        product(0, 0)
+        product(0, 0, 128)
+        product(0, 128, 128)
+        divide("vector", 0, 0, 128)
+        divide("scalar", 0, 128, 128)
+        store(0, 0, 256)
         rows_to_columns(nc.scalar.copy, e_tiles[3][:], e_grouped, 3)
-        product(0, 1)
-        divide(0, 0, True)
-        store(0, slice(0, HALF))
-        divide(0, 1, False)
-        store(0, slice(HALF, E))
+        product(0, 256, 256)
+        divide("scalar", 0, 256, 256)
+        store(0, 256, 256)
         quantise_e(2)
         invert_sums(2, 2)
-        product(1, 0)
-        product(1, 1)
-        divide(1, 0, True)
-        divide(1, 1, False)
-        store(1, slice(0, E))
+        product(1, 0, 256)
+        product(1, 256, 256)
+        divide("vector", 1, 0, 256)
+        divide("scalar", 1, 256, 256)
+        store(1, 0, 512)
         quantise_e(3)
-        product(2, 0)
-        product(2, 1)
-        divide(2, 0, True)
-        divide(2, 1, False)
-        store(2, slice(0, E))
-        product(3, 0)
-        product(3, 1)
-        divide(3, 0, True)
-        divide(3, 1, False)
-        store(3, slice(0, E))
+        product(2, 0, 256)
+        product(2, 256, 256)
+        divide("vector", 2, 0, 256)
+        divide("scalar", 2, 256, 256)
+        store(2, 0, 512)
+        product(3, 0, 256)
+        product(3, 256, 256)
+        divide("vector", 3, 0, 256)
+        divide("scalar", 3, 256, 256)
+        store(3, 0, 512)

@@ -50,10 +50,10 @@ def tile_sparseattention_s_kernel(tc, q, k, v, out):
         k_sb = keep.tile([P, TILES, E], BF16)
         q_sb = keep.tile([P, TILES, E], BF16)
         v_sb = keep.tile([P, PACK, E], BF16)
-        for first, n in ((0, 1), (1, 1), (2, 1), (3, 1)):
-            nc.sync.dma_start(out=k_sb[:, first : first + n], in_=k_rows[:, first : first + n])
         for first, n in ((0, 1), (1, 1), (2, 2)):
-            nc.sync.dma_start(out=q_sb[:, first : first + n], in_=q_rows[:, first : first + n])
+            nc.sync.dma_start(out=k_sb[:, first : first + n], in_=k_rows[:, first : first + n])
+        for i in range(TILES):
+            nc.sync.dma_start(out=q_sb[:, i], in_=q_rows[:, i])
         for b in range(STRIDE):
             nc.sync.dma_start(
                 out=v_sb[b:P:STRIDE].rearrange("g t f -> g (t f)"), in_=v_rows[b]

@@ -50,7 +50,7 @@ def tile_sparseattention_s_kernel(tc, q, k, v, out):
         k_sb = keep.tile([P, TILES, E], BF16)
         q_sb = keep.tile([P, TILES, E], BF16)
         v_sb = keep.tile([P, PACK, E], BF16)
-        for first, n in ((0, 1), (1, 1), (2, 2)):
+        for first, n in ((0, 2), (2, 1), (3, 1)):
             nc.sync.dma_start(out=k_sb[:, first : first + n], in_=k_rows[:, first : first + n])
         for i in range(TILES):
             nc.sync.dma_start(out=q_sb[:, i], in_=q_rows[:, i])

import math
from contextlib import ExitStack

import concourse.mybir as mybir
from concourse.masks import make_identity

F32 = mybir.dt.float32
BF16 = mybir.dt.bfloat16
U32 = mybir.dt.uint32
U8 = mybir.dt.uint8
FP8X4 = mybir.dt.float8_e4m3fn_x4
ACT = mybir.ActivationFunctionType
ALU = mybir.AluOpType

P = 128
PACK = 4
PAIR = 2
T = 512
E = 512
HEADS = 16
TILES = T // P
STRIDE = 4
ROW_WORDS = E // PAIR
WORD_TILES = ROW_WORDS // P
OUT_HALVES = 2
HALF = E // OUT_HALVES
SCALAR_FEATS = 192
PSUM_BANKS = 8
WARM_UP = 3
GPSIMD_FEATS = ((0, HALF), (HALF, E - HALF - SCALAR_FEATS))
SCALE = 1.0 / math.sqrt(E // HEADS)

FLOPS = 2 * 2 * T * T * E


def tile_sparseattention_s_kernel(tc, q, k, v, out):
    nc = tc.nc
    q_rows = q.flatten_outer_dims().rearrange("(p t) f -> p t f", t=TILES)
    k_rows = k.flatten_outer_dims().rearrange("(p t) f -> p t f", t=TILES)
    out_rows = out.flatten_outer_dims().rearrange("(p t) f -> p t f", t=TILES)
    v_rows = v.flatten_outer_dims().rearrange("(b g t) f -> b g (t f)", b=STRIDE, t=PACK)

    with ExitStack() as ctx:
        keep = ctx.enter_context(tc.tile_pool(name="keep", bufs=1))
        work = ctx.enter_context(tc.tile_pool(name="work", bufs=TILES))
        idle_psum = ctx.enter_context(tc.psum_pool(name="idle_psum", bufs=1))
        psum = ctx.enter_context(tc.psum_pool(name="psum", bufs=PSUM_BANKS - 1))
        ctx.enter_context(tc.manual_schedule())

        k_sb = keep.tile([P, TILES, E], BF16)
        q_sb = keep.tile([P, TILES, E], BF16)
        v_sb = keep.tile([P, PACK, E], BF16)
        for first, n in ((0, 2), (2, 1), (3, 1)):
            nc.sync.dma_start(out=k_sb[:, first : first + n], in_=k_rows[:, first : first + n])
        for i in range(TILES):
            nc.sync.dma_start(out=q_sb[:, i], in_=q_rows[:, i])
        for b in range(STRIDE):
            nc.sync.dma_start(
                out=v_sb[b:P:STRIDE].rearrange("g t f -> g (t f)"), in_=v_rows[b]
            )

        ident = keep.tile([P, P], F32)
        make_identity(nc, ident[:])

        zeros = keep.tile([P, P], F32)
        nc.vector.memset(zeros[:], 0.0)

        one = keep.tile([P, 1], F32)
        nc.scalar.activation(out=one[:], in_=zeros[:, 0:1], func=ACT.Exp)

        idle = idle_psum.tile([P, P], F32)

        def idle_matmul(n_cols):
            nc.tensor.matmul(
                idle[:, :n_cols], lhsT=zeros[:], rhs=zeros[:, :n_cols], start=True, stop=True
            )

        words = zeros[:].bitcast(BF16)
        nc.tensor.matmul(idle[:], lhsT=words[:, :P], rhs=words[:, :P], start=True, stop=True)
        nc.tensor.matmul(idle[:], lhsT=words[:, :P], rhs=words[:, P:], start=True, stop=True)
        for i in range(WARM_UP):
            idle_matmul(P)

        k_grouped = keep.tile([P, T * PACK], BF16, align_bytes=64)
        k_codes = keep.tile([P, T], U32, align_bytes=64)
        k_scales = keep.tile([P, T], U8, align_bytes=64)
        q_grouped = keep.tile([P, T * PACK], BF16, align_bytes=64, tag="q_then_gate")
        q_codes = keep.tile([P, T], U32, align_bytes=64)
        q_scales = keep.tile([P, T], U8, align_bytes=64)
        e_grouped = keep.tile([P, T * PACK], BF16, align_bytes=64)
        e_codes = keep.tile([P, T], U32, align_bytes=64)
        e_scales = keep.tile([P, T], U8, align_bytes=64)
        v_grouped = keep.tile([P, E, PACK], BF16, align_bytes=64)
        v_codes = keep.tile([P, E], U32, align_bytes=64)
        v_scales = keep.tile([P, E], U8, align_bytes=64)

        def quantise(grouped, codes, scales, first_col, n_cols):
            nc.vector.quantize_mx(
                out=codes[:, first_col : first_col + n_cols].bitcast(FP8X4),
                scales=scales[:, first_col : first_col + n_cols],
                in_=grouped[:, first_col * PACK : (first_col + n_cols) * PACK],
            )

        def transpose_words(bank_part, rows):
            words = rows.bitcast(F32)
            for w in range(WORD_TILES):
                nc.tensor.transpose(bank_part[:, w, :], words[:, w * P : (w + 1) * P], ident[:])

        def rows_to_columns(copy, rows, grouped, i):
            bank = psum.tile([P, WORD_TILES, P], F32, tag="bank")
            transpose_words(bank, rows)
            dst = grouped[:].bitcast(F32)[:, i * P * WORD_TILES : (i + 1) * P * WORD_TILES]
            copy(
                out=dst.rearrange("p (r w) -> p r w", w=WORD_TILES),
                in_=bank[:].rearrange("p w r -> p r w"),
            )

        def keys_to_columns(copy, t):
            bank = psum.tile([P, WORD_TILES, P], F32, tag="bank")
            transpose_words(bank, k_sb[:, t, :])
            dst = k_grouped[:].bitcast(F32)[:, t * P * WORD_TILES : (t + 1) * P * WORD_TILES]
            copy(
                out=dst.rearrange("p (g b w) -> p g b w", b=STRIDE, w=WORD_TILES),
                in_=bank[:].rearrange("p w (b g) -> p g b w", b=STRIDE),
            )

        for b in range(TILES):
            keys_to_columns((nc.vector.tensor_copy, nc.scalar.copy)[b % 2], b)
        for u in range(TILES // PAIR):
            quantise(k_grouped, k_codes, k_scales, u * PAIR * P, PAIR * P)
        for i in range(TILES):
            rows_to_columns(nc.scalar.copy, q_sb[:, i, :], q_grouped, i)
            quantise(q_grouped, q_codes, q_scales, i * P, P)

        gate = keep.tile([P, 1], BF16, align_bytes=64, tag="q_then_gate")
        nc.gpsimd.memset(gate[:], 0.0)
        for first, n in GPSIMD_FEATS:
            feats = slice(first, first + n)
            nc.gpsimd.tensor_scalar(
                out=v_grouped[:, feats, :],
                in0=v_sb[:, :, feats].rearrange("l b f -> l f b"),
                scalar1=1.0,
                scalar2=0.0,
                op0=ALU.mult,
                op1=ALU.add,
            )
        nc.scalar.copy(
            out=v_grouped[:, E - SCALAR_FEATS :, :],
            in_=v_sb[:, :, E - SCALAR_FEATS :].rearrange("l b f -> l f b"),
        )

        def quantise_v(first, n):
            feats = slice(first, first + n)
            nc.vector.quantize_mx(
                out=v_codes[:, feats].bitcast(FP8X4),
                scales=v_scales[:, feats],
                in_=v_grouped[:, feats, :].rearrange("l f b -> l (f b)"),
            )

        e_tiles = []
        row_sums = keep.tile([P, TILES], F32)
        for i in range(TILES):
            cols = slice(i * P, (i + 1) * P)
            s = psum.tile([P, T], F32, tag="bank")
            nc.tensor.matmul_mx(
                out=s[:],
                lhsT=q_codes[:, cols].bitcast(FP8X4),
                lhsT_scale=q_scales[:, cols],
                rhs=k_codes[:].bitcast(FP8X4),
                rhs_scale=k_scales[:],
                start=True,
                stop=True,
            )
            scaled = work.tile([P, T], F32)
            bias = work.tile([P, 1], F32)
            nc.vector.tensor_scalar(
                out=scaled[:],
                in0=s[:],
                scalar1=-SCALE,
                scalar2=None,
                op0=ALU.mult,
                op1=ALU.min,
                accum_out=bias[:],
            )
            e = work.tile([P, T], BF16)
            nc.scalar.activation(
                out=e[:].rearrange("p (u l c) -> p u l c", u=T // (PAIR * P), c=PAIR),
                in_=s[:].rearrange("p (u c l) -> p u l c", u=T // (PAIR * P), c=PAIR),
                func=ACT.Exp,
                bias=bias[:],
                scale=SCALE,
                accum_out=row_sums[:, i : i + 1],
            )
            e_tiles.append(e)

        inv_sums = keep.tile([P, TILES], F32)

        def invert_sums(first, n):
            nc.vector.reciprocal(inv_sums[:, first : first + n], row_sums[:, first : first + n])

        o_banks = {}

        def product(i, first, n):
            cols = slice(i * P, (i + 1) * P)
            feats = slice(first, first + n)
            o = psum.tile([P, HALF], F32, tag="bank")
            nc.tensor.matmul_mx(
                out=o[:, :n],
                lhsT=e_codes[:, cols].bitcast(FP8X4),
                lhsT_scale=e_scales[:, cols],
                rhs=v_codes[:, feats].bitcast(FP8X4),
                rhs_scale=v_scales[:, feats],
                start=True,
                stop=True,
            )
            o_banks[i, first] = o

        def quantise_e(i):
            quantise(e_grouped, e_codes, e_scales, i * P, P)

        o_sb = []
        for i in range(TILES):
            o_tile = work.tile([P, E], F32)
            o_sb.append(o_tile)

        def divide(engine, i, first, n):
            out_cols = o_sb[i][:, first : first + n]
            inv_sum = inv_sums[:, i : i + 1]
            if engine == "vector":
                nc.vector.tensor_tensor(
                    out=out_cols,
                    in0=o_banks[i, first][:, :n],
                    in1=inv_sum.to_broadcast([P, n]),
                    op=ALU.mult,
                )
            else:
                nc.scalar.activation(
                    out=out_cols, in_=o_banks[i, first][:, :n], func=ACT.Copy, scale=inv_sum
                )

        def store(i, first, n):
            feats = slice(first, first + n)
            nc.sync.dma_start(out=out_rows[:, i, feats], in_=o_sb[i][:, feats])

        idle_matmul(128)
        rows_to_columns(nc.vector.tensor_copy, e_tiles[0][:], e_grouped, 0)
        idle_matmul(64)
        quantise_v(0, 128)
        quantise_e(0)
        invert_sums(0, 2)
        rows_to_columns(nc.scalar.copy, e_tiles[1][:], e_grouped, 1)
        idle_matmul(64)
        quantise_v(128, 128)
        quantise_v(256, 256)
        quantise_e(1)
        rows_to_columns(nc.scalar.copy, e_tiles[2][:], e_grouped, 2)
        idle_matmul(64)
        product(0, 0, 128)
        product(0, 128, 128)
        divide("vector", 0, 0, 128)
        divide("scalar", 0, 128, 128)
        store(0, 0, 256)
        rows_to_columns(nc.scalar.copy, e_tiles[3][:], e_grouped, 3)
        product(0, 256, 256)
        divide("scalar", 0, 256, 256)
        store(0, 256, 256)
        quantise_e(2)
        invert_sums(2, 2)
        product(1, 0, 256)
        product(1, 256, 256)
        divide("vector", 1, 0, 256)
        divide("scalar", 1, 256, 256)
        store(1, 0, 512)
        quantise_e(3)
        product(2, 0, 256)
        product(2, 256, 256)
        divide("vector", 2, 0, 256)
        divide("scalar", 2, 256, 256)
        store(2, 0, 512)
        product(3, 0, 256)
        product(3, 256, 256)
        divide("vector", 3, 0, 256)
        divide("scalar", 3, 256, 256)
        store(3, 0, 512)
